import numpy as np
import ml_dtypes


def mxq(x, axis, fmt="e4m3"):
    dtype, down = {"e4m3": (ml_dtypes.float8_e4m3fn, 7), "e5m2": (ml_dtypes.float8_e5m2, 14)}[fmt]
    v = np.moveaxis(np.asarray(x, np.float32).astype(ml_dtypes.bfloat16).astype(np.float64), axis, -1)
    blocks = v.reshape(v.shape[:-1] + (-1, 32))
    amax = np.abs(blocks).max(-1, keepdims=True)
    byte = np.maximum(np.where(amax > 0, np.frexp(amax)[1] - 1 + 127, 0) - down, 1)
    scale = np.exp2(byte - 127.0)
    codes = (blocks / scale).astype(np.float32).astype(dtype).astype(np.float64)
    return np.moveaxis((codes * scale).reshape(v.shape), -1, axis)


WIDE = False


def mx_kscale(k):
    if not WIDE:
        return np.ones(k)
    levels = np.array([10, -10, 5, -5, 0])
    a = np.random.permutation(np.resize(levels, k // 512 * 4)).reshape(k // 512, 4)
    idx = np.arange(k)
    return np.exp2(a[idx // 512, idx % 128 // 32])


BF16 = ml_dtypes.bfloat16


def bf(x):
    return np.asarray(x, np.float32).astype(BF16)


def f64(x):
    return np.asarray(x).astype(np.float64)


E2M1 = np.array([0.0, 0.5, 1.0, 1.5, 2.0, 3.0, 4.0, 6.0, -0.0, -0.5, -1.0, -1.5, -2.0, -3.0, -4.0, -6.0])


def pack_weight(w, fmt):
    k, n = w.shape
    w = f64(bf(w)).reshape(k // 32, 32, n)
    amax = np.abs(w).max(1)
    if fmt == "e4m3":
        byte = np.frexp(amax)[1] - 1 + 127 - 7
    else:
        mant, ex = np.frexp(amax / 6.0)
        byte = np.where(mant > 0.5, ex, ex - 1) + 127
    byte = np.clip(np.where(amax > 0, byte, 1), 1, 254)
    scaled = (w * np.exp2(127.0 - byte)[:, None, :]).reshape(k, n).astype(np.float32)
    by_word = np.ascontiguousarray(scaled.reshape(k // 512, 128, 4, n).transpose(0, 1, 3, 2))
    if fmt == "e4m3":
        words = by_word.astype(ml_dtypes.float8_e4m3fn).view(np.uint8)
    else:
        c = by_word.astype(ml_dtypes.float4_e2m1fn).view(np.uint8) & 0xF
        words = c[..., 0::2] | (c[..., 1::2] << 4)
    return np.ascontiguousarray(words), np.ascontiguousarray(byte.astype(np.uint8).reshape(k // 512, 16, n))


def unpack_weight(words, scales, fmt):
    g, p, n, _ = words.shape
    if fmt == "e4m3":
        vals = np.ascontiguousarray(words).view(ml_dtypes.float8_e4m3fn).astype(np.float64)
    else:
        nib = np.empty((g, p, n, 4), np.uint8)
        nib[..., 0::2] = words & 0xF
        nib[..., 1::2] = words >> 4
        vals = E2M1[nib]
    vals = vals * np.repeat(np.exp2(scales.astype(np.float64) - 127.0), 8, axis=1)[..., None]
    return vals.transpose(0, 1, 3, 2).reshape(g * 512, n)


B, N_VAR, D = 128, 2, 2048
NUM_UNITS = N_VAR * D
ONE = 1


def sigmoid(v):
    return 1.0 / (1.0 + np.exp(-v))


def setup_inputs():
    s = mx_kscale(D)
    inputs = bf(np.random.standard_normal((B, N_VAR)))
    hidden = bf((np.random.standard_normal((B, D, N_VAR)) * s[None, :, None]).reshape(B, NUM_UNITS))
    gate_w_I2H = bf(np.random.standard_normal((N_VAR, 1, 2 * D, 1)) * 0.5)
    gate_stack = (np.random.standard_normal((N_VAR, 1, 2 * D, D)) / np.sqrt(D) / s).swapaxes(-1, -2)
    gate_words, gate_scales = pack_weight(gate_stack.reshape(-1, 2 * D), "e4m3")
    gate_bias = bf(np.random.standard_normal(2 * NUM_UNITS) * 0.4)
    update_w_I2H = bf(np.random.standard_normal((N_VAR, 1, D, 1)) * 0.5)
    update_stack = (np.random.standard_normal((N_VAR, 1, D, D)) * 1.5 / np.sqrt(D) / s).swapaxes(-1, -2)
    update_words, update_scales = pack_weight(update_stack.reshape(-1, D), "e4m3")
    update_bias = bf(np.random.standard_normal(NUM_UNITS) * 0.4)
    return {
        "inputs": inputs,
        "hidden": hidden,
        "gate_w_I2H": gate_w_I2H,
        "gate_w_H2H_words": gate_words,
        "gate_w_H2H_scales": gate_scales,
        "gate_bias": gate_bias,
        "update_w_I2H": update_w_I2H,
        "update_w_H2H_words": update_words,
        "update_w_H2H_scales": update_scales,
        "update_bias": update_bias,
    }


def reference(inputs, hidden, gate_w_I2H, gate_w_H2H_words, gate_w_H2H_scales, gate_bias, update_w_I2H, update_w_H2H_words, update_w_H2H_scales, update_bias):
    inputs, hidden = f64(inputs), f64(hidden)
    b, num_units = hidden.shape
    n_var = inputs.shape[1]
    d = num_units // n_var

    x_v = inputs.T
    h_v = hidden.reshape(b, d, n_var).transpose(2, 0, 1)

    gx = x_v[:, :, None] * f64(gate_w_I2H)[:, 0, :, 0][:, None, :]
    gh = mxq(h_v, 2, "e4m3") @ unpack_weight(gate_w_H2H_words, gate_w_H2H_scales, "e4m3").reshape(n_var, ONE, d, 2 * d)[:, 0]
    res_gate = (gx + gh).transpose(1, 0, 2).reshape(b, 2 * num_units) + f64(gate_bias)
    z, r = res_gate[:, :num_units], res_gate[:, num_units:]

    r_v = sigmoid(r).reshape(b, d, n_var).transpose(2, 0, 1)

    ux = x_v[:, :, None] * f64(update_w_I2H)[:, 0, :, 0][:, None, :]
    uh = mxq(h_v * r_v, 2, "e4m3") @ unpack_weight(update_w_H2H_words, update_w_H2H_scales, "e4m3").reshape(n_var, ONE, d, d)[:, 0]
    g = (ux + uh).transpose(1, 0, 2).reshape(b, num_units) + f64(update_bias)

    zs = sigmoid(z)
    return zs * hidden + (1.0 - zs) * np.tanh(g)

@@ -1,0 +1,265 @@
+from contextlib import ExitStack
+
+import concourse.mybir as mybir
+from concourse.masks import make_identity
+
+F32 = mybir.dt.float32
+BF16 = mybir.dt.bfloat16
+I32 = mybir.dt.int32
+U32 = mybir.dt.uint32
+U8 = mybir.dt.uint8
+FP8X4 = mybir.dt.float8_e4m3fn_x4
+ALU = mybir.AluOpType
+ACT = mybir.ActivationFunctionType
+
+P = 128
+PACK = 4
+K_PASS = P * PACK
+N_VAR = 2
+D = 2048
+UNITS = N_VAR * D
+GROUPS = D // K_PASS
+BANK = 512
+RANGE = 2048
+BLOCKS = RANGE // BANK
+HALVES = UNITS // RANGE
+QUADRANTS = 4
+LIVE = 16
+
+W_BUFS = 10
+AHEAD = W_BUFS - 1
+
+FLOPS = 2 * P * (N_VAR * D * UNITS + N_VAR * D * D)
+
+
+def tile_grucell_w_e_kernel(
+    tc,
+    inputs,
+    hidden,
+    gate_w_I2H,
+    gate_w_H2H_words,
+    gate_w_H2H_scales,
+    gate_bias,
+    update_w_I2H,
+    update_w_H2H_words,
+    update_w_H2H_scales,
+    update_bias,
+    out,
+):
+    nc = tc.nc
+    with ExitStack() as ctx:
+        const = ctx.enter_context(tc.tile_pool(name="const", bufs=1))
+        weights = ctx.enter_context(tc.tile_pool(name="weights", bufs=W_BUFS))
+        work = ctx.enter_context(tc.tile_pool(name="work", bufs=4))
+        psum_mx = ctx.enter_context(tc.psum_pool(name="psum_mx", bufs=4))
+        psum_aux = ctx.enter_context(tc.psum_pool(name="psum_aux", bufs=4))
+
+        gate_planes = [
+            const.tile([P, UNITS], U8, name="gate_planes%d" % v, align_bytes=64) for v in range(N_VAR)
+        ]
+        update_planes = [
+            const.tile([P, D], U8, name="update_planes%d" % v, align_bytes=64) for v in range(N_VAR)
+        ]
+        hidden_sb = const.tile([P, UNITS], BF16, name="hidden_sb")
+        nc.sync.dma_start(out=hidden_sb[:], in_=hidden)
+
+        def load_planes(planes, scales, v):
+            nc.vector.memset(planes[:].bitcast(I32), 0)
+            for quad in range(QUADRANTS):
+                nc.sync.dma_start(
+                    out=planes[32 * quad : 32 * quad + LIVE, :].bitcast(I32),
+                    in_=scales[GROUPS * v : GROUPS * (v + 1), PACK * quad : PACK * (quad + 1), :].bitcast(I32),
+                )
+
+        load_planes(gate_planes[1], gate_w_H2H_scales, 1)
+        load_planes(gate_planes[0], gate_w_H2H_scales, 0)
+        load_planes(update_planes[0], update_w_H2H_scales, 0)
+        load_planes(update_planes[1], update_w_H2H_scales, 1)
+
+        def gate_words(v, half, g):
+            rows = gate_w_H2H_words[GROUPS * v + g].rearrange("p n t -> p (n t)")
+            return rows[:, PACK * RANGE * half : PACK * RANGE * (half + 1)].bitcast(I32)
+
+        def update_words(v, block):
+            rows = update_w_H2H_words[GROUPS * v : GROUPS * (v + 1)].rearrange("g p n t -> p g (n t)")
+            return rows[:, :, PACK * BANK * block : PACK * BANK * (block + 1)].bitcast(I32)
+
+        stream = [gate_words(v, half, g) for v in (1, 0) for half in range(HALVES) for g in range(GROUPS)]
+        stream.extend([update_words(v, block) for v in range(N_VAR) for block in range(BLOCKS)])
+        loaded = []
+
+        def start_load(k):
+            w = weights.tile([P, GROUPS * BANK], U32, name="w", align_bytes=64)
+            view = w[:].bitcast(I32)
+            if stream[k].ndim == 3:
+                view = view.rearrange("p (g n) -> p g n", g=GROUPS)
+            nc.sync.dma_start(out=view, in_=stream[k])
+            loaded.append(w)
+
+        def weights_of(k):
+            if k + AHEAD < len(stream):
+                start_load(k + AHEAD)
+            return loaded[k]
+
+        for k in range(AHEAD):
+            start_load(k)
+
+        range_variable = [v for v in range(N_VAR) for half in range(HALVES)] + [v for v in range(N_VAR)]
+        n_ranges = len(range_variable)
+        gate_ranges = N_VAR * HALVES
+
+        side_rows = const.tile([P, RANGE], BF16, name="side_rows")
+        nc.vector.memset(side_rows[:], 0.0)
+        nc.scalar.dma_start(
+            out=side_rows[0:gate_ranges, :],
+            in_=gate_w_I2H.rearrange("v o (s c) u -> (v o s) (c u)", c=RANGE),
+        )
+        nc.scalar.dma_start(
+            out=side_rows[gate_ranges:n_ranges, :],
+            in_=update_w_I2H.rearrange("v o c u -> (v o) (c u)"),
+        )
+        nc.scalar.dma_start(
+            out=side_rows[n_ranges : n_ranges + gate_ranges, :],
+            in_=gate_bias.rearrange("(s c) -> s c", c=RANGE),
+        )
+        nc.scalar.dma_start(
+            out=side_rows[n_ranges + gate_ranges : 2 * n_ranges, :],
+            in_=update_bias.rearrange("(s c) -> s c", c=RANGE),
+        )
+        x_sb = const.tile([P, N_VAR], BF16, name="x_sb")
+        nc.scalar.dma_start(out=x_sb[:], in_=inputs)
+
+        ident = const.tile([P, P], BF16, name="ident")
+        make_identity(nc, ident[:])
+
+        x_and_one = const.tile([P, n_ranges, P], BF16, name="x_and_one")
+        nc.vector.memset(x_and_one[:], 0.0)
+        for i, v in enumerate(range_variable):
+            nc.vector.tensor_copy(out=x_and_one[:, i, i : i + 1], in_=x_sb[:, v : v + 1])
+            nc.vector.memset(x_and_one[:, i, n_ranges + i : n_ranges + i + 1], 1.0)
+        side_ps = psum_aux.tile([P, n_ranges, P], BF16, name="side_ps", tag="aux")
+        for i in range(n_ranges):
+            nc.tensor.transpose(side_ps[:, i, :], x_and_one[:, i, :], ident[:])
+        side_lhsT = const.tile([P, n_ranges, P], BF16, name="side_lhsT")
+        nc.scalar.copy(out=side_lhsT[:], in_=side_ps[:])
+
+        def side_term(i, block):
+            bank = psum_aux.tile([P, BANK], F32, name="side_bank", tag="aux")
+            nc.tensor.matmul(
+                out=bank[:],
+                lhsT=side_lhsT[:, i, :],
+                rhs=side_rows[:, BANK * block : BANK * (block + 1)],
+                start=True,
+                stop=True,
+            )
+            side = work.tile([P, BANK], F32, name="side")
+            nc.scalar.copy(out=side[:], in_=bank[:])
+            return side
+
+        def quantise_pair(sorted_units, v, pair, codes, scales):
+            turned = psum_aux.tile([P, 2, PACK, P], BF16, name="turned", tag="aux")
+            for g in range(2):
+                for t in range(PACK):
+                    nc.tensor.transpose(turned[:, g, t, :], sorted_units[:, v, 2 * pair + g, t, :], ident[:])
+            grouped = work.tile([P, 2, P, PACK], BF16, name="grouped", align_bytes=64)
+            nc.scalar.copy(out=grouped[:], in_=turned[:].rearrange("p g t b -> p g b t"))
+            cols = slice(2 * pair * P, 2 * (pair + 1) * P)
+            nc.vector.quantize_mx(
+                out=codes[:, v, cols].bitcast(FP8X4),
+                scales=scales[:, v, cols],
+                in_=grouped[:].rearrange("p g b t -> p (g b t)"),
+            )
+
+        h_sorted = const.tile([P, N_VAR, GROUPS, PACK, P], BF16, name="h_sorted")
+        h_codes = const.tile([P, N_VAR, GROUPS * P], U32, name="h_codes", align_bytes=64)
+        h_scales = const.tile([P, N_VAR, GROUPS * P], U8, name="h_scales", align_bytes=64)
+        hr_sorted = const.tile([P, N_VAR, GROUPS, PACK, P], BF16, name="hr_sorted")
+        hr_codes = const.tile([P, N_VAR, GROUPS * P], U32, name="hr_codes", align_bytes=64)
+        hr_scales = const.tile([P, N_VAR, GROUPS * P], U8, name="hr_scales", align_bytes=64)
+
+        hidden_by_word = hidden_sb[:].rearrange("b (g p t v) -> b v g t p", g=GROUPS, p=P, t=PACK)
+        for v in (1, 0):
+            nc.vector.tensor_copy(out=h_sorted[:, v], in_=hidden_by_word[:, v])
+            for pair in range(GROUPS // 2):
+                quantise_pair(h_sorted, v, pair, h_codes, h_scales)
+
+        def mx_pass(acc, codes, scales, v, g, w_cols, plane_cols):
+            nc.tensor.matmul_mx(
+                out=acc[:],
+                lhsT=codes[:, v, g * P : (g + 1) * P].bitcast(FP8X4),
+                lhsT_scale=scales[:, v, g * P : (g + 1) * P],
+                rhs=w_cols.bitcast(FP8X4),
+                rhs_scale=plane_cols,
+                start=(g == 0),
+                stop=(g == GROUPS - 1),
+            )
+
+        def gate_range(first_load, v, half):
+            sides = [side_term(HALVES * v + half, block) for block in range(BLOCKS)]
+            accs = [psum_mx.tile([P, BANK], F32, name="acc") for block in range(BLOCKS)]
+            for g in range(GROUPS):
+                w = weights_of(first_load + g)
+                for block in range(BLOCKS):
+                    col = RANGE * half + BANK * block
+                    mx_pass(
+                        accs[block], h_codes, h_scales, v, g,
+                        w[:, BANK * block : BANK * (block + 1)],
+                        gate_planes[v][PACK * g : P, col : col + BANK],
+                    )
+            gates = []
+            for block in range(BLOCKS):
+                pre = work.tile([P, BANK], F32, name="pre")
+                nc.vector.tensor_tensor(out=pre[:], in0=accs[block][:], in1=sides[block][:], op=ALU.add)
+                gate = work.tile([P, BANK], F32, name="gate")
+                nc.scalar.activation(out=gate[:], in_=pre[:], func=ACT.Sigmoid)
+                gates.append(gate)
+            return gates
+
+        half_p = BANK // (PACK * N_VAR)
+        for half in range(HALVES):
+            gates = gate_range(GROUPS * half, 1, half)
+            for block in range(BLOCKS):
+                bank = BLOCKS * half + block
+                g = bank * half_p // P
+                p0 = bank * half_p % P
+                nc.vector.tensor_tensor(
+                    out=hr_sorted[:, :, g, :, p0 : p0 + half_p],
+                    in0=h_sorted[:, :, g, :, p0 : p0 + half_p],
+                    in1=gates[block][:].rearrange("b (p t v) -> b v t p", t=PACK, v=N_VAR),
+                    op=ALU.mult,
+                )
+            for v in range(N_VAR):
+                quantise_pair(hr_sorted, v, half, hr_codes, hr_scales)
+
+        keep = const.tile([P, UNITS], F32, name="keep")
+        fresh = const.tile([P, UNITS], F32, name="fresh")
+        for half in range(HALVES):
+            gates = gate_range(GROUPS * (HALVES + half), 0, half)
+            for block in range(BLOCKS):
+                cols = slice(RANGE * half + BANK * block, RANGE * half + BANK * (block + 1))
+                nc.vector.tensor_tensor(out=keep[:, cols], in0=gates[block][:], in1=hidden_sb[:, cols], op=ALU.mult)
+                nc.vector.tensor_scalar(
+                    out=fresh[:, cols], in0=gates[block][:], scalar1=-1.0, scalar2=1.0, op0=ALU.mult, op1=ALU.add
+                )
+
+        for v in range(N_VAR):
+            for block in range(BLOCKS):
+                cols = slice(D * v + BANK * block, D * v + BANK * (block + 1))
+                side = side_term(gate_ranges + v, block)
+                w = weights_of(GROUPS * HALVES * N_VAR + BLOCKS * v + block)
+                acc = psum_mx.tile([P, BANK], F32, name="acc")
+                for g in range(GROUPS):
+                    mx_pass(
+                        acc, hr_codes, hr_scales, v, g,
+                        w[:, BANK * g : BANK * (g + 1)],
+                        update_planes[v][PACK * g : P, BANK * block : BANK * (block + 1)],
+                    )
+                pre = work.tile([P, BANK], F32, name="pre")
+                nc.vector.tensor_tensor(out=pre[:], in0=acc[:], in1=side[:], op=ALU.add)
+                cand = work.tile([P, BANK], F32, name="cand")
+                nc.scalar.activation(out=cand[:], in_=pre[:], func=ACT.Tanh)
+                mixed = work.tile([P, BANK], F32, name="mixed")
+                nc.vector.tensor_tensor(out=mixed[:], in0=cand[:], in1=fresh[:, cols], op=ALU.mult)
+                result = work.tile([P, BANK], F32, name="result")
+                nc.vector.tensor_tensor(out=result[:], in0=mixed[:], in1=keep[:, cols], op=ALU.add)
+                nc.sync.dma_start(out=out[:, cols], in_=result[:])

@@ -48,44 +48,41 @@ def tile_grucell_w_e_kernel(
 ):
     nc = tc.nc
     with ExitStack() as ctx:
+        ctx.enter_context(tc.manual_schedule())
         const = ctx.enter_context(tc.tile_pool(name="const", bufs=1))
         weights = ctx.enter_context(tc.tile_pool(name="weights", bufs=W_BUFS))
         work = ctx.enter_context(tc.tile_pool(name="work", bufs=4))
-        psum_mx = ctx.enter_context(tc.psum_pool(name="psum_mx", bufs=4))
+        psum_mx = ctx.enter_context(tc.psum_pool(name="psum_mx", bufs=BLOCKS))
         psum_aux = ctx.enter_context(tc.psum_pool(name="psum_aux", bufs=4))
 
-        gate_planes = [
-            const.tile([P, UNITS], U8, name="gate_planes%d" % v, align_bytes=64) for v in range(N_VAR)
-        ]
-        update_planes = [
-            const.tile([P, D], U8, name="update_planes%d" % v, align_bytes=64) for v in range(N_VAR)
-        ]
         hidden_sb = const.tile([P, UNITS], BF16, name="hidden_sb")
         nc.sync.dma_start(out=hidden_sb[:], in_=hidden)
 
-        def load_planes(planes, scales, v):
+        def load_planes(name, scales, v):
+            planes = const.tile([P, scales.shape[2]], U8, name=name, align_bytes=64)
             nc.vector.memset(planes[:].bitcast(I32), 0)
             for quad in range(QUADRANTS):
                 nc.sync.dma_start(
                     out=planes[32 * quad : 32 * quad + LIVE, :].bitcast(I32),
                     in_=scales[GROUPS * v : GROUPS * (v + 1), PACK * quad : PACK * (quad + 1), :].bitcast(I32),
                 )
+            return planes
 
-        load_planes(gate_planes[1], gate_w_H2H_scales, 1)
-        load_planes(gate_planes[0], gate_w_H2H_scales, 0)
-        load_planes(update_planes[0], update_w_H2H_scales, 0)
-        load_planes(update_planes[1], update_w_H2H_scales, 1)
+        reset_planes = load_planes("reset_planes", gate_w_H2H_scales, 1)
+        update_planes = load_planes("update_planes", gate_w_H2H_scales, 0)
+        gate_planes = [update_planes, reset_planes]
+        cand_planes = [load_planes("cand_planes%d" % v, update_w_H2H_scales, v) for v in range(N_VAR)]
 
         def gate_words(v, half, g):
             rows = gate_w_H2H_words[GROUPS * v + g].rearrange("p n t -> p (n t)")
             return rows[:, PACK * RANGE * half : PACK * RANGE * (half + 1)].bitcast(I32)
 
-        def update_words(v, block):
+        def cand_words(v, block):
             rows = update_w_H2H_words[GROUPS * v : GROUPS * (v + 1)].rearrange("g p n t -> p g (n t)")
             return rows[:, :, PACK * BANK * block : PACK * BANK * (block + 1)].bitcast(I32)
 
         stream = [gate_words(v, half, g) for v in (1, 0) for half in range(HALVES) for g in range(GROUPS)]
-        stream.extend([update_words(v, block) for v in range(N_VAR) for block in range(BLOCKS)])
+        stream.extend([cand_words(v, block) for v in range(N_VAR) for block in range(BLOCKS)])
         loaded = []
 
         def start_load(k):
@@ -96,9 +93,12 @@ def tile_grucell_w_e_kernel(
             nc.sync.dma_start(out=view, in_=stream[k])
             loaded.append(w)
 
-        def weights_of(k):
-            if k + AHEAD < len(stream):
-                start_load(k + AHEAD)
+        def next_weights():
+            k = len(loaded) - AHEAD
+            if len(loaded) < len(stream):
+                start_load(len(loaded))
+            else:
+                loaded.append(None)
             return loaded[k]
 
         for k in range(AHEAD):
@@ -108,6 +108,8 @@ def tile_grucell_w_e_kernel(
         n_ranges = len(range_variable)
         gate_ranges = N_VAR * HALVES
 
+        x_sb = const.tile([P, N_VAR], BF16, name="x_sb")
+        nc.scalar.dma_start(out=x_sb[:], in_=inputs)
         side_rows = const.tile([P, RANGE], BF16, name="side_rows")
         nc.vector.memset(side_rows[:], 0.0)
         nc.scalar.dma_start(
@@ -126,8 +128,6 @@ def tile_grucell_w_e_kernel(
             out=side_rows[n_ranges + gate_ranges : 2 * n_ranges, :],
             in_=update_bias.rearrange("(s c) -> s c", c=RANGE),
         )
-        x_sb = const.tile([P, N_VAR], BF16, name="x_sb")
-        nc.scalar.dma_start(out=x_sb[:], in_=inputs)
 
         ident = const.tile([P, P], BF16, name="ident")
         make_identity(nc, ident[:])
@@ -143,25 +143,28 @@ def tile_grucell_w_e_kernel(
         side_lhsT = const.tile([P, n_ranges, P], BF16, name="side_lhsT")
         nc.scalar.copy(out=side_lhsT[:], in_=side_ps[:])
 
-        def side_term(i, block):
-            bank = psum_aux.tile([P, BANK], F32, name="side_bank", tag="aux")
-            nc.tensor.matmul(
-                out=bank[:],
-                lhsT=side_lhsT[:, i, :],
-                rhs=side_rows[:, BANK * block : BANK * (block + 1)],
-                start=True,
-                stop=True,
-            )
-            side = work.tile([P, BANK], F32, name="side")
-            nc.scalar.copy(out=side[:], in_=bank[:])
-            return side
+        def side_terms(i):
+            sides = []
+            for block in range(BLOCKS):
+                bank = psum_aux.tile([P, BANK], F32, name="side_bank", tag="aux")
+                nc.tensor.matmul(
+                    out=bank[:],
+                    lhsT=side_lhsT[:, i, :],
+                    rhs=side_rows[:, BANK * block : BANK * (block + 1)],
+                    start=True,
+                    stop=True,
+                )
+                side = work.tile([P, BANK], F32, name="side", bufs=2 * BLOCKS)
+                nc.scalar.copy(out=side[:], in_=bank[:])
+                sides.append(side)
+            return sides
 
         def quantise_pair(sorted_units, v, pair, codes, scales):
             turned = psum_aux.tile([P, 2, PACK, P], BF16, name="turned", tag="aux")
             for g in range(2):
                 for t in range(PACK):
                     nc.tensor.transpose(turned[:, g, t, :], sorted_units[:, v, 2 * pair + g, t, :], ident[:])
-            grouped = work.tile([P, 2, P, PACK], BF16, name="grouped", align_bytes=64)
+            grouped = work.tile([P, 2, P, PACK], BF16, name="grouped", bufs=2, align_bytes=64)
             nc.scalar.copy(out=grouped[:], in_=turned[:].rearrange("p g t b -> p g b t"))
             cols = slice(2 * pair * P, 2 * (pair + 1) * P)
             nc.vector.quantize_mx(
@@ -180,6 +183,7 @@ def tile_grucell_w_e_kernel(
         hidden_by_word = hidden_sb[:].rearrange("b (g p t v) -> b v g t p", g=GROUPS, p=P, t=PACK)
         for v in (1, 0):
             nc.vector.tensor_copy(out=h_sorted[:, v], in_=hidden_by_word[:, v])
+        for v in (1, 0):
             for pair in range(GROUPS // 2):
                 quantise_pair(h_sorted, v, pair, h_codes, h_scales)
 
@@ -194,11 +198,15 @@ def tile_grucell_w_e_kernel(
                 stop=(g == GROUPS - 1),
             )
 
-        def gate_range(first_load, v, half):
-            sides = [side_term(HALVES * v + half, block) for block in range(BLOCKS)]
+        def add_side(acc, side):
+            pre = work.tile([P, BANK], F32, name="pre", bufs=BLOCKS + 2)
+            nc.vector.tensor_tensor(out=pre[:], in0=acc[:], in1=side[:], op=ALU.add)
+            return pre
+
+        def gate_range(v, half, sides):
             accs = [psum_mx.tile([P, BANK], F32, name="acc") for block in range(BLOCKS)]
             for g in range(GROUPS):
-                w = weights_of(first_load + g)
+                w = next_weights()
                 for block in range(BLOCKS):
                     col = RANGE * half + BANK * block
                     mx_pass(
@@ -206,60 +214,78 @@ def tile_grucell_w_e_kernel(
                         w[:, BANK * block : BANK * (block + 1)],
                         gate_planes[v][PACK * g : P, col : col + BANK],
                     )
-            gates = []
-            for block in range(BLOCKS):
-                pre = work.tile([P, BANK], F32, name="pre")
-                nc.vector.tensor_tensor(out=pre[:], in0=accs[block][:], in1=sides[block][:], op=ALU.add)
-                gate = work.tile([P, BANK], F32, name="gate")
-                nc.scalar.activation(out=gate[:], in_=pre[:], func=ACT.Sigmoid)
-                gates.append(gate)
-            return gates
+            return [add_side(accs[block], sides[block]) for block in range(BLOCKS)]
 
-        half_p = BANK // (PACK * N_VAR)
-        for half in range(HALVES):
-            gates = gate_range(GROUPS * half, 1, half)
+        def activated(pre, func, scale):
+            act = work.tile([P, BANK], F32, name="act")
+            nc.scalar.activation(out=act[:], in_=pre[:], func=func, scale=scale)
+            return act
+
+        bank_p = BANK // (PACK * N_VAR)
+
+        def reset_product(half, pres):
             for block in range(BLOCKS):
+                reset = activated(pres[block], ACT.Sigmoid, 1.0)
                 bank = BLOCKS * half + block
-                g = bank * half_p // P
-                p0 = bank * half_p % P
+                g = bank * bank_p // P
+                p0 = bank * bank_p % P
                 nc.vector.tensor_tensor(
-                    out=hr_sorted[:, :, g, :, p0 : p0 + half_p],
-                    in0=h_sorted[:, :, g, :, p0 : p0 + half_p],
-                    in1=gates[block][:].rearrange("b (p t v) -> b v t p", t=PACK, v=N_VAR),
+                    out=hr_sorted[:, :, g, :, p0 : p0 + bank_p],
+                    in0=h_sorted[:, :, g, :, p0 : p0 + bank_p],
+                    in1=reset[:].rearrange("b (p t v) -> b v t p", t=PACK, v=N_VAR),
                     op=ALU.mult,
                 )
+
+        def quantise_product(pair):
             for v in range(N_VAR):
-                quantise_pair(hr_sorted, v, half, hr_codes, hr_scales)
+                quantise_pair(hr_sorted, v, pair, hr_codes, hr_scales)
 
         keep = const.tile([P, UNITS], F32, name="keep")
         fresh = const.tile([P, UNITS], F32, name="fresh")
-        for half in range(HALVES):
-            gates = gate_range(GROUPS * (HALVES + half), 0, half)
+
+        def update_gate(half, pres):
             for block in range(BLOCKS):
                 cols = slice(RANGE * half + BANK * block, RANGE * half + BANK * (block + 1))
-                nc.vector.tensor_tensor(out=keep[:, cols], in0=gates[block][:], in1=hidden_sb[:, cols], op=ALU.mult)
-                nc.vector.tensor_scalar(
-                    out=fresh[:, cols], in0=gates[block][:], scalar1=-1.0, scalar2=1.0, op0=ALU.mult, op1=ALU.add
-                )
+                update = activated(pres[block], ACT.Sigmoid, 1.0)
+                nc.vector.tensor_tensor(out=keep[:, cols], in0=update[:], in1=hidden_sb[:, cols], op=ALU.mult)
+            for block in range(BLOCKS):
+                cols = slice(RANGE * half + BANK * block, RANGE * half + BANK * (block + 1))
+                nc.scalar.activation(out=fresh[:, cols], in_=pres[block][:], func=ACT.Sigmoid, scale=-1.0)
 
+        sides_r0 = side_terms(HALVES)
+        sides_r1 = side_terms(HALVES + 1)
+        reset_product(0, gate_range(1, 0, sides_r0))
+        sides_z0 = side_terms(0)
+        reset_product(1, gate_range(1, 1, sides_r1))
+        quantise_product(0)
+        sides_z1 = side_terms(1)
+        update_gate(0, gate_range(0, 0, sides_z0))
+        quantise_product(1)
+        cand_sides = [side_terms(gate_ranges)]
+        update_gate(1, gate_range(0, 1, sides_z1))
+        cand_sides.append(side_terms(gate_ranges + 1))
+
+        def blend(cols, cand):
+            mixed = work.tile([P, BANK], F32, name="mixed", bufs=2)
+            nc.vector.tensor_tensor(out=mixed[:], in0=cand[:], in1=fresh[:, cols], op=ALU.mult)
+            result = work.tile([P, BANK], F32, name="result", bufs=3)
+            nc.vector.tensor_tensor(out=result[:], in0=mixed[:], in1=keep[:, cols], op=ALU.add)
+            nc.sync.dma_start(out=out[:, cols], in_=result[:])
+
+        waiting = []
         for v in range(N_VAR):
             for block in range(BLOCKS):
-                cols = slice(D * v + BANK * block, D * v + BANK * (block + 1))
-                side = side_term(gate_ranges + v, block)
-                w = weights_of(GROUPS * HALVES * N_VAR + BLOCKS * v + block)
+                w = next_weights()
                 acc = psum_mx.tile([P, BANK], F32, name="acc")
                 for g in range(GROUPS):
                     mx_pass(
                         acc, hr_codes, hr_scales, v, g,
                         w[:, BANK * g : BANK * (g + 1)],
-                        update_planes[v][PACK * g : P, BANK * block : BANK * (block + 1)],
+                        cand_planes[v][PACK * g : P, BANK * block : BANK * (block + 1)],
                     )
-                pre = work.tile([P, BANK], F32, name="pre")
-                nc.vector.tensor_tensor(out=pre[:], in0=acc[:], in1=side[:], op=ALU.add)
-                cand = work.tile([P, BANK], F32, name="cand")
-                nc.scalar.activation(out=cand[:], in_=pre[:], func=ACT.Tanh)
-                mixed = work.tile([P, BANK], F32, name="mixed")
-                nc.vector.tensor_tensor(out=mixed[:], in0=cand[:], in1=fresh[:, cols], op=ALU.mult)
-                result = work.tile([P, BANK], F32, name="result")
-                nc.vector.tensor_tensor(out=result[:], in0=mixed[:], in1=keep[:, cols], op=ALU.add)
-                nc.sync.dma_start(out=out[:, cols], in_=result[:])
+                cand = activated(add_side(acc, cand_sides[v][block]), ACT.Tanh, 1.0)
+                for cols, earlier in waiting:
+                    blend(cols, earlier)
+                waiting = [(slice(D * v + BANK * block, D * v + BANK * (block + 1)), cand)]
+        for cols, earlier in waiting:
+            blend(cols, earlier)

@@ -28,6 +28,7 @@ LIVE = 16
 
 W_BUFS = 10
 AHEAD = W_BUFS - 1
+SIDE_BUFS = 4 * BLOCKS
 
 FLOPS = 2 * P * (N_VAR * D * UNITS + N_VAR * D * D)
 
@@ -57,14 +58,16 @@ def tile_grucell_w_e_kernel(
 
         hidden_sb = const.tile([P, UNITS], BF16, name="hidden_sb")
         nc.sync.dma_start(out=hidden_sb[:], in_=hidden)
+        ident = const.tile([P, P], BF16, name="ident")
+        make_identity(nc, ident[:])
 
         def load_planes(name, scales, v):
             planes = const.tile([P, scales.shape[2]], U8, name=name, align_bytes=64)
             nc.vector.memset(planes[:].bitcast(I32), 0)
             for quad in range(QUADRANTS):
-                nc.sync.dma_start(
-                    out=planes[32 * quad : 32 * quad + LIVE, :].bitcast(I32),
-                    in_=scales[GROUPS * v : GROUPS * (v + 1), PACK * quad : PACK * (quad + 1), :].bitcast(I32),
+                nc.gpsimd.dma_start(
+                    out=planes[32 * quad : 32 * quad + LIVE, :].bitcast(F32),
+                    in_=scales[GROUPS * v : GROUPS * (v + 1), PACK * quad : PACK * (quad + 1), :].bitcast(F32),
                 )
             return planes
 
@@ -129,9 +132,6 @@ def tile_grucell_w_e_kernel(
             in_=update_bias.rearrange("(s c) -> s c", c=RANGE),
         )
 
-        ident = const.tile([P, P], BF16, name="ident")
-        make_identity(nc, ident[:])
-
         x_and_one = const.tile([P, n_ranges, P], BF16, name="x_and_one")
         nc.vector.memset(x_and_one[:], 0.0)
         for i, v in enumerate(range_variable):
@@ -143,21 +143,26 @@ def tile_grucell_w_e_kernel(
         side_lhsT = const.tile([P, n_ranges, P], BF16, name="side_lhsT")
         nc.scalar.copy(out=side_lhsT[:], in_=side_ps[:])
 
-        def side_terms(i):
-            sides = []
-            for block in range(BLOCKS):
-                bank = psum_aux.tile([P, BANK], F32, name="side_bank", tag="aux")
-                nc.tensor.matmul(
-                    out=bank[:],
-                    lhsT=side_lhsT[:, i, :],
-                    rhs=side_rows[:, BANK * block : BANK * (block + 1)],
-                    start=True,
-                    stop=True,
-                )
-                side = work.tile([P, BANK], F32, name="side", bufs=2 * BLOCKS)
-                nc.scalar.copy(out=side[:], in_=bank[:])
-                sides.append(side)
-            return sides
+        sides = {}
+
+        def side_term(i, block):
+            bank = psum_aux.tile([P, BANK], F32, name="side_bank", tag="aux")
+            nc.tensor.matmul(
+                out=bank[:],
+                lhsT=side_lhsT[:, i, :],
+                rhs=side_rows[:, BANK * block : BANK * (block + 1)],
+                start=True,
+                stop=True,
+            )
+            side = work.tile([P, BANK], F32, name="side", bufs=SIDE_BUFS)
+            nc.scalar.copy(out=side[:], in_=bank[:])
+            sides[(i, block)] = side
+
+        side_order = [(i, block) for i in (2, 3, 0, 1, 4, 5) for block in range(BLOCKS)]
+
+        def next_side_terms(count):
+            for i, block in side_order[len(sides) : len(sides) + count]:
+                side_term(i, block)
 
         def quantise_pair(sorted_units, v, pair, codes, scales):
             turned = psum_aux.tile([P, 2, PACK, P], BF16, name="turned", tag="aux")
@@ -182,8 +187,11 @@ def tile_grucell_w_e_kernel(
 
         hidden_by_word = hidden_sb[:].rearrange("b (g p t v) -> b v g t p", g=GROUPS, p=P, t=PACK)
         for v in (1, 0):
-            nc.vector.tensor_copy(out=h_sorted[:, v], in_=hidden_by_word[:, v])
-        for v in (1, 0):
+            for pair in range(GROUPS // 2):
+                groups = slice(2 * pair, 2 * (pair + 1))
+                nc.vector.tensor_copy(out=h_sorted[:, v, groups], in_=hidden_by_word[:, v, groups])
+
+        def quantise_hidden(v):
             for pair in range(GROUPS // 2):
                 quantise_pair(h_sorted, v, pair, h_codes, h_scales)
 
@@ -203,7 +211,7 @@ def tile_grucell_w_e_kernel(
             nc.vector.tensor_tensor(out=pre[:], in0=acc[:], in1=side[:], op=ALU.add)
             return pre
 
-        def gate_range(v, half, sides):
+        def gate_range(v, half):
             accs = [psum_mx.tile([P, BANK], F32, name="acc") for block in range(BLOCKS)]
             for g in range(GROUPS):
                 w = next_weights()
@@ -214,7 +222,8 @@ def tile_grucell_w_e_kernel(
                         w[:, BANK * block : BANK * (block + 1)],
                         gate_planes[v][PACK * g : P, col : col + BANK],
                     )
-            return [add_side(accs[block], sides[block]) for block in range(BLOCKS)]
+                next_side_terms(2)
+            return [add_side(accs[block], sides[(HALVES * v + half, block)]) for block in range(BLOCKS)]
 
         def activated(pre, func, scale):
             act = work.tile([P, BANK], F32, name="act")
@@ -252,18 +261,15 @@ def tile_grucell_w_e_kernel(
                 cols = slice(RANGE * half + BANK * block, RANGE * half + BANK * (block + 1))
                 nc.scalar.activation(out=fresh[:, cols], in_=pres[block][:], func=ACT.Sigmoid, scale=-1.0)
 
-        sides_r0 = side_terms(HALVES)
-        sides_r1 = side_terms(HALVES + 1)
-        reset_product(0, gate_range(1, 0, sides_r0))
-        sides_z0 = side_terms(0)
-        reset_product(1, gate_range(1, 1, sides_r1))
+        quantise_hidden(1)
+        next_side_terms(BLOCKS)
+        reset_product(0, gate_range(1, 0))
+        quantise_hidden(0)
+        reset_product(1, gate_range(1, 1))
         quantise_product(0)
-        sides_z1 = side_terms(1)
-        update_gate(0, gate_range(0, 0, sides_z0))
+        update_gate(0, gate_range(0, 0))
         quantise_product(1)
-        cand_sides = [side_terms(gate_ranges)]
-        update_gate(1, gate_range(0, 1, sides_z1))
-        cand_sides.append(side_terms(gate_ranges + 1))
+        update_gate(1, gate_range(0, 1))
 
         def blend(cols, cand):
             mixed = work.tile([P, BANK], F32, name="mixed", bufs=2)
@@ -283,7 +289,7 @@ def tile_grucell_w_e_kernel(
                         w[:, BANK * g : BANK * (g + 1)],
                         cand_planes[v][PACK * g : P, BANK * block : BANK * (block + 1)],
                     )
-                cand = activated(add_side(acc, cand_sides[v][block]), ACT.Tanh, 1.0)
+                cand = activated(add_side(acc, sides[(gate_ranges + v, block)]), ACT.Tanh, 1.0)
                 for cols, earlier in waiting:
                     blend(cols, earlier)
                 waiting = [(slice(D * v + BANK * block, D * v + BANK * (block + 1)), cand)]

@@ -274,9 +274,8 @@ def tile_grucell_w_e_kernel(
         def blend(cols, cand):
             mixed = work.tile([P, BANK], F32, name="mixed", bufs=2)
             nc.vector.tensor_tensor(out=mixed[:], in0=cand[:], in1=fresh[:, cols], op=ALU.mult)
-            result = work.tile([P, BANK], F32, name="result", bufs=3)
-            nc.vector.tensor_tensor(out=result[:], in0=mixed[:], in1=keep[:, cols], op=ALU.add)
-            nc.sync.dma_start(out=out[:, cols], in_=result[:])
+            nc.vector.tensor_tensor(out=keep[:, cols], in0=mixed[:], in1=keep[:, cols], op=ALU.add)
+            nc.sync.dma_start(out=out[:, cols], in_=keep[:, cols])
 
         waiting = []
         for v in range(N_VAR):

@@ -28,6 +28,7 @@ LIVE = 16
 
 W_BUFS = 10
 AHEAD = W_BUFS - 1
+FIRST_LOADS = 2
 SIDE_BUFS = 4 * BLOCKS
 
 FLOPS = 2 * P * (N_VAR * D * UNITS + N_VAR * D * D)
@@ -57,24 +58,29 @@ def tile_grucell_w_e_kernel(
         psum_aux = ctx.enter_context(tc.psum_pool(name="psum_aux", bufs=4))
 
         hidden_sb = const.tile([P, UNITS], BF16, name="hidden_sb")
-        nc.sync.dma_start(out=hidden_sb[:], in_=hidden)
+        for half in range(HALVES):
+            nc.sync.dma_start(
+                out=hidden_sb[:, RANGE * half : RANGE * (half + 1)], in_=hidden[:, RANGE * half : RANGE * (half + 1)]
+            )
         ident = const.tile([P, P], BF16, name="ident")
         make_identity(nc, ident[:])
 
-        def load_planes(name, scales, v):
+        def load_planes(name, scales, v, in_front):
             planes = const.tile([P, scales.shape[2]], U8, name=name, align_bytes=64)
             nc.vector.memset(planes[:].bitcast(I32), 0)
             for quad in range(QUADRANTS):
-                nc.gpsimd.dma_start(
-                    out=planes[32 * quad : 32 * quad + LIVE, :].bitcast(F32),
-                    in_=scales[GROUPS * v : GROUPS * (v + 1), PACK * quad : PACK * (quad + 1), :].bitcast(F32),
-                )
+                dst = planes[32 * quad : 32 * quad + LIVE, :]
+                src = scales[GROUPS * v : GROUPS * (v + 1), PACK * quad : PACK * (quad + 1), :]
+                if in_front:
+                    nc.sync.dma_start(out=dst.bitcast(I32), in_=src.bitcast(I32))
+                else:
+                    nc.gpsimd.dma_start(out=dst.bitcast(F32), in_=src.bitcast(F32))
             return planes
 
-        reset_planes = load_planes("reset_planes", gate_w_H2H_scales, 1)
-        update_planes = load_planes("update_planes", gate_w_H2H_scales, 0)
+        reset_planes = load_planes("reset_planes", gate_w_H2H_scales, 1, True)
+        update_planes = load_planes("update_planes", gate_w_H2H_scales, 0, False)
         gate_planes = [update_planes, reset_planes]
-        cand_planes = [load_planes("cand_planes%d" % v, update_w_H2H_scales, v) for v in range(N_VAR)]
+        cand_planes = [load_planes("cand_planes%d" % v, update_w_H2H_scales, v, False) for v in range(N_VAR)]
 
         def gate_words(v, half, g):
             rows = gate_w_H2H_words[GROUPS * v + g].rearrange("p n t -> p (n t)")
@@ -104,7 +110,7 @@ def tile_grucell_w_e_kernel(
                 loaded.append(None)
             return loaded[k]
 
-        for k in range(AHEAD):
+        for k in range(FIRST_LOADS):
             start_load(k)
 
         range_variable = [v for v in range(N_VAR) for half in range(HALVES)] + [v for v in range(N_VAR)]
@@ -112,36 +118,44 @@ def tile_grucell_w_e_kernel(
         gate_ranges = N_VAR * HALVES
 
         x_sb = const.tile([P, N_VAR], BF16, name="x_sb")
-        nc.scalar.dma_start(out=x_sb[:], in_=inputs)
+        nc.sync.dma_start(out=x_sb[:], in_=inputs)
         side_rows = const.tile([P, RANGE], BF16, name="side_rows")
         nc.vector.memset(side_rows[:], 0.0)
-        nc.scalar.dma_start(
+        nc.sync.dma_start(
             out=side_rows[0:gate_ranges, :],
             in_=gate_w_I2H.rearrange("v o (s c) u -> (v o s) (c u)", c=RANGE),
         )
-        nc.scalar.dma_start(
+        nc.sync.dma_start(
             out=side_rows[gate_ranges:n_ranges, :],
             in_=update_w_I2H.rearrange("v o c u -> (v o) (c u)"),
         )
-        nc.scalar.dma_start(
+        nc.sync.dma_start(
             out=side_rows[n_ranges : n_ranges + gate_ranges, :],
             in_=gate_bias.rearrange("(s c) -> s c", c=RANGE),
         )
-        nc.scalar.dma_start(
+        nc.sync.dma_start(
             out=side_rows[n_ranges + gate_ranges : 2 * n_ranges, :],
             in_=update_bias.rearrange("(s c) -> s c", c=RANGE),
         )
 
+        for k in range(FIRST_LOADS, AHEAD):
+            start_load(k)
+
         x_and_one = const.tile([P, n_ranges, P], BF16, name="x_and_one")
         nc.vector.memset(x_and_one[:], 0.0)
-        for i, v in enumerate(range_variable):
-            nc.vector.tensor_copy(out=x_and_one[:, i, i : i + 1], in_=x_sb[:, v : v + 1])
-            nc.vector.memset(x_and_one[:, i, n_ranges + i : n_ranges + i + 1], 1.0)
-        side_ps = psum_aux.tile([P, n_ranges, P], BF16, name="side_ps", tag="aux")
         for i in range(n_ranges):
-            nc.tensor.transpose(side_ps[:, i, :], x_and_one[:, i, :], ident[:])
+            nc.vector.memset(x_and_one[:, i, n_ranges + i : n_ranges + i + 1], 1.0)
         side_lhsT = const.tile([P, n_ranges, P], BF16, name="side_lhsT")
-        nc.scalar.copy(out=side_lhsT[:], in_=side_ps[:])
+
+        def place_inputs():
+            for i, v in enumerate(range_variable):
+                nc.vector.tensor_copy(out=x_and_one[:, i, i : i + 1], in_=x_sb[:, v : v + 1])
+
+        def turn_inputs():
+            side_ps = psum_aux.tile([P, n_ranges, P], BF16, name="side_ps", tag="aux")
+            for i in range(n_ranges):
+                nc.tensor.transpose(side_ps[:, i, :], x_and_one[:, i, :], ident[:])
+            nc.scalar.copy(out=side_lhsT[:], in_=side_ps[:])
 
         sides = {}
 
@@ -186,7 +200,8 @@ def tile_grucell_w_e_kernel(
         hr_scales = const.tile([P, N_VAR, GROUPS * P], U8, name="hr_scales", align_bytes=64)
 
         hidden_by_word = hidden_sb[:].rearrange("b (g p t v) -> b v g t p", g=GROUPS, p=P, t=PACK)
-        for v in (1, 0):
+
+        def sort_hidden(v):
             for pair in range(GROUPS // 2):
                 groups = slice(2 * pair, 2 * (pair + 1))
                 nc.vector.tensor_copy(out=h_sorted[:, v, groups], in_=hidden_by_word[:, v, groups])
@@ -211,7 +226,10 @@ def tile_grucell_w_e_kernel(
             nc.vector.tensor_tensor(out=pre[:], in0=acc[:], in1=side[:], op=ALU.add)
             return pre
 
-        def gate_range(v, half):
+        def two_side_terms(g):
+            next_side_terms(2)
+
+        def gate_range(v, half, after_group=two_side_terms):
             accs = [psum_mx.tile([P, BANK], F32, name="acc") for block in range(BLOCKS)]
             for g in range(GROUPS):
                 w = next_weights()
@@ -222,7 +240,7 @@ def tile_grucell_w_e_kernel(
                         w[:, BANK * block : BANK * (block + 1)],
                         gate_planes[v][PACK * g : P, col : col + BANK],
                     )
-                next_side_terms(2)
+                after_group(g)
             return [add_side(accs[block], sides[(HALVES * v + half, block)]) for block in range(BLOCKS)]
 
         def activated(pre, func, scale):
@@ -261,9 +279,17 @@ def tile_grucell_w_e_kernel(
                 cols = slice(RANGE * half + BANK * block, RANGE * half + BANK * (block + 1))
                 nc.scalar.activation(out=fresh[:, cols], in_=pres[block][:], func=ACT.Sigmoid, scale=-1.0)
 
+        def first_side_terms(g):
+            if g == 1:
+                turn_inputs()
+            if g >= 2:
+                next_side_terms(BLOCKS)
+
+        sort_hidden(1)
         quantise_hidden(1)
-        next_side_terms(BLOCKS)
-        reset_product(0, gate_range(1, 0))
+        place_inputs()
+        sort_hidden(0)
+        reset_product(0, gate_range(1, 0, first_side_terms))
         quantise_hidden(0)
         reset_product(1, gate_range(1, 1))
         quantise_product(0)

@@ -62,6 +62,8 @@ def tile_grucell_w_e_kernel(
             nc.sync.dma_start(
                 out=hidden_sb[:, RANGE * half : RANGE * (half + 1)], in_=hidden[:, RANGE * half : RANGE * (half + 1)]
             )
+        ident_words = const.tile([P, P], F32, name="ident_words")
+        make_identity(nc, ident_words[:])
         ident = const.tile([P, P], BF16, name="ident")
         make_identity(nc, ident[:])
 
@@ -178,43 +180,31 @@ def tile_grucell_w_e_kernel(
             for i, block in side_order[len(sides) : len(sides) + count]:
                 side_term(i, block)
 
-        def quantise_pair(sorted_units, v, pair, codes, scales):
-            turned = psum_aux.tile([P, 2, PACK, P], BF16, name="turned", tag="aux")
-            for g in range(2):
-                for t in range(PACK):
-                    nc.tensor.transpose(turned[:, g, t, :], sorted_units[:, v, 2 * pair + g, t, :], ident[:])
-            grouped = work.tile([P, 2, P, PACK], BF16, name="grouped", bufs=2, align_bytes=64)
-            nc.scalar.copy(out=grouped[:], in_=turned[:].rearrange("p g t b -> p g b t"))
-            cols = slice(2 * pair * P, 2 * (pair + 1) * P)
+        def quantise_group(units, g, codes, scales, copier):
+            words = units[:].bitcast(F32)
+            turned = psum_aux.tile([P, PACK, P], F32, name="turned", tag="aux")
+            for t in range(PACK):
+                nc.tensor.transpose(turned[:, t, :], words[:, K_PASS * g + t : K_PASS * (g + 1) : PACK], ident_words[:])
+            grouped = work.tile([P, N_VAR, P, PACK], BF16, name="grouped", bufs=2, align_bytes=64)
+            halves = turned[:].rearrange("p t b -> p (t b)").bitcast(BF16)
+            copier(out=grouped[:], in_=halves.rearrange("p (t b v) -> p v b t", t=PACK, v=N_VAR))
             nc.vector.quantize_mx(
-                out=codes[:, v, cols].bitcast(FP8X4),
-                scales=scales[:, v, cols],
-                in_=grouped[:].rearrange("p g b t -> p (g b t)"),
+                out=codes[:, g, :].bitcast(FP8X4),
+                scales=scales[:, g, :],
+                in_=grouped[:].rearrange("p v b t -> p (v b t)"),
             )
 
-        h_sorted = const.tile([P, N_VAR, GROUPS, PACK, P], BF16, name="h_sorted")
-        h_codes = const.tile([P, N_VAR, GROUPS * P], U32, name="h_codes", align_bytes=64)
-        h_scales = const.tile([P, N_VAR, GROUPS * P], U8, name="h_scales", align_bytes=64)
-        hr_sorted = const.tile([P, N_VAR, GROUPS, PACK, P], BF16, name="hr_sorted")
-        hr_codes = const.tile([P, N_VAR, GROUPS * P], U32, name="hr_codes", align_bytes=64)
-        hr_scales = const.tile([P, N_VAR, GROUPS * P], U8, name="hr_scales", align_bytes=64)
-
-        hidden_by_word = hidden_sb[:].rearrange("b (g p t v) -> b v g t p", g=GROUPS, p=P, t=PACK)
-
-        def sort_hidden(v):
-            for pair in range(GROUPS // 2):
-                groups = slice(2 * pair, 2 * (pair + 1))
-                nc.vector.tensor_copy(out=h_sorted[:, v, groups], in_=hidden_by_word[:, v, groups])
-
-        def quantise_hidden(v):
-            for pair in range(GROUPS // 2):
-                quantise_pair(h_sorted, v, pair, h_codes, h_scales)
+        h_codes = const.tile([P, GROUPS, N_VAR * P], U32, name="h_codes", align_bytes=64)
+        h_scales = const.tile([P, GROUPS, N_VAR * P], U8, name="h_scales", align_bytes=64)
+        hr = const.tile([P, UNITS], BF16, name="hr")
+        hr_codes = const.tile([P, GROUPS, N_VAR * P], U32, name="hr_codes", align_bytes=64)
+        hr_scales = const.tile([P, GROUPS, N_VAR * P], U8, name="hr_scales", align_bytes=64)
 
         def mx_pass(acc, codes, scales, v, g, w_cols, plane_cols):
             nc.tensor.matmul_mx(
                 out=acc[:],
-                lhsT=codes[:, v, g * P : (g + 1) * P].bitcast(FP8X4),
-                lhsT_scale=scales[:, v, g * P : (g + 1) * P],
+                lhsT=codes[:, g, v * P : (v + 1) * P].bitcast(FP8X4),
+                lhsT_scale=scales[:, g, v * P : (v + 1) * P],
                 rhs=w_cols.bitcast(FP8X4),
                 rhs_scale=plane_cols,
                 start=(g == 0),
@@ -248,24 +238,15 @@ def tile_grucell_w_e_kernel(
             nc.scalar.activation(out=act[:], in_=pre[:], func=func, scale=scale)
             return act
 
-        bank_p = BANK // (PACK * N_VAR)
-
         def reset_product(half, pres):
             for block in range(BLOCKS):
                 reset = activated(pres[block], ACT.Sigmoid, 1.0)
-                bank = BLOCKS * half + block
-                g = bank * bank_p // P
-                p0 = bank * bank_p % P
-                nc.vector.tensor_tensor(
-                    out=hr_sorted[:, :, g, :, p0 : p0 + bank_p],
-                    in0=h_sorted[:, :, g, :, p0 : p0 + bank_p],
-                    in1=reset[:].rearrange("b (p t v) -> b v t p", t=PACK, v=N_VAR),
-                    op=ALU.mult,
-                )
+                cols = slice(RANGE * half + BANK * block, RANGE * half + BANK * (block + 1))
+                nc.vector.tensor_tensor(out=hr[:, cols], in0=hidden_sb[:, cols], in1=reset[:], op=ALU.mult)
 
         def quantise_product(pair):
-            for v in range(N_VAR):
-                quantise_pair(hr_sorted, v, pair, hr_codes, hr_scales)
+            for g in (2 * pair, 2 * pair + 1):
+                quantise_group(hr, g, hr_codes, hr_scales, nc.scalar.copy)
 
         keep = const.tile([P, UNITS], F32, name="keep")
         fresh = const.tile([P, UNITS], F32, name="fresh")
@@ -285,12 +266,10 @@ def tile_grucell_w_e_kernel(
             if g >= 2:
                 next_side_terms(BLOCKS)
 
-        sort_hidden(1)
-        quantise_hidden(1)
+        for g in range(GROUPS):
+            quantise_group(hidden_sb, g, h_codes, h_scales, nc.scalar.copy if g % 2 == 0 else nc.vector.tensor_copy)
         place_inputs()
-        sort_hidden(0)
         reset_product(0, gate_range(1, 0, first_side_terms))
-        quantise_hidden(0)
         reset_product(1, gate_range(1, 1))
         quantise_product(0)
         update_gate(0, gate_range(0, 0))

@@ -23,6 +23,8 @@ BANK = 512
 RANGE = 2048
 BLOCKS = RANGE // BANK
 HALVES = UNITS // RANGE
+QUARTER = 2 * BANK
+QUARTERS = UNITS // QUARTER
 QUADRANTS = 4
 LIVE = 16
 
@@ -93,14 +95,21 @@ def tile_grucell_w_e_kernel(
             return rows[:, :, PACK * BANK * block : PACK * BANK * (block + 1)].bitcast(I32)
 
         stream = [gate_words(v, half, g) for v in (1, 0) for half in range(HALVES) for g in range(GROUPS)]
-        stream.extend([cand_words(v, block) for v in range(N_VAR) for block in range(BLOCKS)])
+        def quarter_words(q, s):
+            first = GROUPS * (q // 2) + 2 * s
+            rows = update_w_H2H_words[first : first + 2].rearrange("g p n t -> p g (n t)")
+            col = QUARTER * (q % 2)
+            return rows[:, :, PACK * col : PACK * (col + QUARTER)].bitcast(I32)
+
+        stream.extend([quarter_words(q, s) for q in range(QUARTERS - 1) for s in range(2)])
+        stream.extend([cand_words(1, block) for block in (2, 3)])
         loaded = []
 
         def start_load(k):
             w = weights.tile([P, GROUPS * BANK], U32, name="w", align_bytes=64)
             view = w[:].bitcast(I32)
             if stream[k].ndim == 3:
-                view = view.rearrange("p (g n) -> p g n", g=GROUPS)
+                view = view.rearrange("p (g n) -> p g n", g=stream[k].shape[1])
             nc.sync.dma_start(out=view, in_=stream[k])
             loaded.append(w)
 
@@ -282,9 +291,39 @@ def tile_grucell_w_e_kernel(
             nc.vector.tensor_tensor(out=keep[:, cols], in0=mixed[:], in1=keep[:, cols], op=ALU.add)
             nc.sync.dma_start(out=out[:, cols], in_=keep[:, cols])
 
+        def candidate_quarter(q):
+            v = q // 2
+            accs = [psum_mx.tile([P, BANK], F32, name="acc") for block in range(2)]
+            for s in range(2):
+                w = next_weights()
+                for g in (2 * s, 2 * s + 1):
+                    for block in range(2):
+                        first = QUARTER * (g % 2) + BANK * block
+                        col = QUARTER * (q % 2) + BANK * block
+                        mx_pass(
+                            accs[block], hr_codes, hr_scales, v, g,
+                            w[:, first : first + BANK],
+                            cand_planes[v][PACK * g : P, col : col + BANK],
+                        )
+            pres = [add_side(accs[block], sides[(gate_ranges + v, 2 * (q % 2) + block)]) for block in range(2)]
+            cands = [activated(pres[block], ACT.Tanh, 1.0) for block in range(2)]
+            mixeds = []
+            for block in range(2):
+                cols = slice(QUARTER * q + BANK * block, QUARTER * q + BANK * (block + 1))
+                mixed = work.tile([P, BANK], F32, name="mixed", bufs=2)
+                nc.vector.tensor_tensor(out=mixed[:], in0=cands[block][:], in1=fresh[:, cols], op=ALU.mult)
+                mixeds.append(mixed)
+            for block in range(2):
+                cols = slice(QUARTER * q + BANK * block, QUARTER * q + BANK * (block + 1))
+                nc.vector.tensor_tensor(out=keep[:, cols], in0=mixeds[block][:], in1=keep[:, cols], op=ALU.add)
+            nc.sync.dma_start(out=out[:, QUARTER * q : QUARTER * (q + 1)], in_=keep[:, QUARTER * q : QUARTER * (q + 1)])
+
+        for q in range(QUARTERS - 1):
+            candidate_quarter(q)
+
         waiting = []
-        for v in range(N_VAR):
-            for block in range(BLOCKS):
+        for v in (1,):
+            for block in (2, 3):
                 w = next_weights()
                 acc = psum_mx.tile([P, BANK], F32, name="acc")
                 for g in range(GROUPS):

@@ -66,8 +66,6 @@ def tile_grucell_w_e_kernel(
             )
         ident_words = const.tile([P, P], F32, name="ident_words")
         make_identity(nc, ident_words[:])
-        ident = const.tile([P, P], BF16, name="ident")
-        make_identity(nc, ident[:])
 
         def load_planes(name, scales, v, in_front):
             planes = const.tile([P, scales.shape[2]], U8, name=name, align_bytes=64)
@@ -81,10 +79,9 @@ def tile_grucell_w_e_kernel(
                     nc.gpsimd.dma_start(out=dst.bitcast(F32), in_=src.bitcast(F32))
             return planes
 
-        reset_planes = load_planes("reset_planes", gate_w_H2H_scales, 1, True)
-        update_planes = load_planes("update_planes", gate_w_H2H_scales, 0, False)
-        gate_planes = [update_planes, reset_planes]
-        cand_planes = [load_planes("cand_planes%d" % v, update_w_H2H_scales, v, False) for v in range(N_VAR)]
+        reset_planes = load_planes("reset_planes", gate_w_H2H_scales, 1, False)
+        ident = const.tile([P, P], BF16, name="ident")
+        make_identity(nc, ident[:])
 
         def gate_words(v, half, g):
             rows = gate_w_H2H_words[GROUPS * v + g].rearrange("p n t -> p (n t)")
@@ -153,12 +150,12 @@ def tile_grucell_w_e_kernel(
             start_load(k)
 
         x_and_one = const.tile([P, n_ranges, P], BF16, name="x_and_one")
-        nc.vector.memset(x_and_one[:], 0.0)
-        for i in range(n_ranges):
-            nc.vector.memset(x_and_one[:, i, n_ranges + i : n_ranges + i + 1], 1.0)
         side_lhsT = const.tile([P, n_ranges, P], BF16, name="side_lhsT")
 
         def place_inputs():
+            nc.vector.memset(x_and_one[:], 0.0)
+            for i in range(n_ranges):
+                nc.vector.memset(x_and_one[:, i, n_ranges + i : n_ranges + i + 1], 1.0)
             for i, v in enumerate(range_variable):
                 nc.vector.tensor_copy(out=x_and_one[:, i, i : i + 1], in_=x_sb[:, v : v + 1])
 
@@ -226,7 +223,7 @@ def tile_grucell_w_e_kernel(
             return pre
 
         def two_side_terms(g):
-            next_side_terms(2)
+            next_side_terms(1)
 
         def gate_range(v, half, after_group=two_side_terms):
             accs = [psum_mx.tile([P, BANK], F32, name="acc") for block in range(BLOCKS)]
@@ -277,6 +274,9 @@ def tile_grucell_w_e_kernel(
 
         for g in range(GROUPS):
             quantise_group(hidden_sb, g, h_codes, h_scales, nc.scalar.copy if g % 2 == 0 else nc.vector.tensor_copy)
+        update_planes = load_planes("update_planes", gate_w_H2H_scales, 0, False)
+        gate_planes = [update_planes, reset_planes]
+        cand_planes = [load_planes("cand_planes%d" % v, update_w_H2H_scales, v, False) for v in range(N_VAR)]
         place_inputs()
         reset_product(0, gate_range(1, 0, first_side_terms))
         reset_product(1, gate_range(1, 1))
@@ -305,6 +305,7 @@ def tile_grucell_w_e_kernel(
                             w[:, first : first + BANK],
                             cand_planes[v][PACK * g : P, col : col + BANK],
                         )
+                next_side_terms(1)
             pres = [add_side(accs[block], sides[(gate_ranges + v, 2 * (q % 2) + block)]) for block in range(2)]
             cands = [activated(pres[block], ACT.Tanh, 1.0) for block in range(2)]
             mixeds = []

from contextlib import ExitStack

import concourse.mybir as mybir
from concourse.masks import make_identity

F32 = mybir.dt.float32
BF16 = mybir.dt.bfloat16
I32 = mybir.dt.int32
U32 = mybir.dt.uint32
U8 = mybir.dt.uint8
FP8X4 = mybir.dt.float8_e4m3fn_x4
ALU = mybir.AluOpType
ACT = mybir.ActivationFunctionType

P = 128
PACK = 4
K_PASS = P * PACK
N_VAR = 2
D = 2048
UNITS = N_VAR * D
GROUPS = D // K_PASS
BANK = 512
RANGE = 2048
BLOCKS = RANGE // BANK
HALVES = UNITS // RANGE
QUARTER = 2 * BANK
QUARTERS = UNITS // QUARTER
QUADRANTS = 4
LIVE = 16

W_BUFS = 10
AHEAD = W_BUFS - 1
FIRST_LOADS = 2
SIDE_BUFS = 4 * BLOCKS

FLOPS = 2 * P * (N_VAR * D * UNITS + N_VAR * D * D)


def tile_grucell_w_e_kernel(
    tc,
    inputs,
    hidden,
    gate_w_I2H,
    gate_w_H2H_words,
    gate_w_H2H_scales,
    gate_bias,
    update_w_I2H,
    update_w_H2H_words,
    update_w_H2H_scales,
    update_bias,
    out,
):
    nc = tc.nc
    with ExitStack() as ctx:
        ctx.enter_context(tc.manual_schedule())
        const = ctx.enter_context(tc.tile_pool(name="const", bufs=1))
        weights = ctx.enter_context(tc.tile_pool(name="weights", bufs=W_BUFS))
        work = ctx.enter_context(tc.tile_pool(name="work", bufs=4))
        psum_mx = ctx.enter_context(tc.psum_pool(name="psum_mx", bufs=BLOCKS))
        psum_aux = ctx.enter_context(tc.psum_pool(name="psum_aux", bufs=4))

        hidden_sb = const.tile([P, UNITS], BF16, name="hidden_sb")
        for half in range(HALVES):
            nc.sync.dma_start(
                out=hidden_sb[:, RANGE * half : RANGE * (half + 1)], in_=hidden[:, RANGE * half : RANGE * (half + 1)]
            )
        ident_words = const.tile([P, P], F32, name="ident_words")
        make_identity(nc, ident_words[:])

        def load_planes(name, scales, v, in_front):
            planes = const.tile([P, scales.shape[2]], U8, name=name, align_bytes=64)
            nc.vector.memset(planes[:].bitcast(I32), 0)
            for quad in range(QUADRANTS):
                dst = planes[32 * quad : 32 * quad + LIVE, :]
                src = scales[GROUPS * v : GROUPS * (v + 1), PACK * quad : PACK * (quad + 1), :]
                if in_front:
                    nc.sync.dma_start(out=dst.bitcast(I32), in_=src.bitcast(I32))
                else:
                    nc.gpsimd.dma_start(out=dst.bitcast(F32), in_=src.bitcast(F32))
            return planes

        reset_planes = load_planes("reset_planes", gate_w_H2H_scales, 1, False)
        ident = const.tile([P, P], BF16, name="ident")
        make_identity(nc, ident[:])

        def gate_words(v, half, g):
            rows = gate_w_H2H_words[GROUPS * v + g].rearrange("p n t -> p (n t)")
            return rows[:, PACK * RANGE * half : PACK * RANGE * (half + 1)].bitcast(I32)

        def cand_words(v, block):
            rows = update_w_H2H_words[GROUPS * v : GROUPS * (v + 1)].rearrange("g p n t -> p g (n t)")
            return rows[:, :, PACK * BANK * block : PACK * BANK * (block + 1)].bitcast(I32)

        stream = [gate_words(v, half, g) for v in (1, 0) for half in range(HALVES) for g in range(GROUPS)]
        def quarter_words(q, s):
            first = GROUPS * (q // 2) + 2 * s
            rows = update_w_H2H_words[first : first + 2].rearrange("g p n t -> p g (n t)")
            col = QUARTER * (q % 2)
            return rows[:, :, PACK * col : PACK * (col + QUARTER)].bitcast(I32)

        stream.extend([quarter_words(q, s) for q in range(QUARTERS - 1) for s in range(2)])
        stream.extend([cand_words(1, block) for block in (2, 3)])
        loaded = []

        def start_load(k):
            w = weights.tile([P, GROUPS * BANK], U32, name="w", align_bytes=64)
            view = w[:].bitcast(I32)
            if stream[k].ndim == 3:
                view = view.rearrange("p (g n) -> p g n", g=stream[k].shape[1])
            nc.sync.dma_start(out=view, in_=stream[k])
            loaded.append(w)

        def next_weights():
            k = len(loaded) - AHEAD
            if len(loaded) < len(stream):
                start_load(len(loaded))
            else:
                loaded.append(None)
            return loaded[k]

        for k in range(FIRST_LOADS):
            start_load(k)

        range_variable = [v for v in range(N_VAR) for half in range(HALVES)] + [v for v in range(N_VAR)]
        n_ranges = len(range_variable)
        gate_ranges = N_VAR * HALVES

        x_sb = const.tile([P, N_VAR], BF16, name="x_sb")
        nc.sync.dma_start(out=x_sb[:], in_=inputs)
        side_rows = const.tile([P, RANGE], BF16, name="side_rows")
        nc.vector.memset(side_rows[:], 0.0)
        nc.sync.dma_start(
            out=side_rows[0:gate_ranges, :],
            in_=gate_w_I2H.rearrange("v o (s c) u -> (v o s) (c u)", c=RANGE),
        )
        nc.sync.dma_start(
            out=side_rows[gate_ranges:n_ranges, :],
            in_=update_w_I2H.rearrange("v o c u -> (v o) (c u)"),
        )
        nc.sync.dma_start(
            out=side_rows[n_ranges : n_ranges + gate_ranges, :],
            in_=gate_bias.rearrange("(s c) -> s c", c=RANGE),
        )
        nc.sync.dma_start(
            out=side_rows[n_ranges + gate_ranges : 2 * n_ranges, :],
            in_=update_bias.rearrange("(s c) -> s c", c=RANGE),
        )

        for k in range(FIRST_LOADS, AHEAD):
            start_load(k)

        x_and_one = const.tile([P, n_ranges, P], BF16, name="x_and_one")
        side_lhsT = const.tile([P, n_ranges, P], BF16, name="side_lhsT")

        def place_inputs():
            nc.vector.memset(x_and_one[:], 0.0)
            for i in range(n_ranges):
                nc.vector.memset(x_and_one[:, i, n_ranges + i : n_ranges + i + 1], 1.0)
            for i, v in enumerate(range_variable):
                nc.vector.tensor_copy(out=x_and_one[:, i, i : i + 1], in_=x_sb[:, v : v + 1])

        def turn_inputs():
            side_ps = psum_aux.tile([P, n_ranges, P], BF16, name="side_ps", tag="aux")
            for i in range(n_ranges):
                nc.tensor.transpose(side_ps[:, i, :], x_and_one[:, i, :], ident[:])
            nc.scalar.copy(out=side_lhsT[:], in_=side_ps[:])

        sides = {}

        def side_term(i, block):
            bank = psum_aux.tile([P, BANK], F32, name="side_bank", tag="aux")
            nc.tensor.matmul(
                out=bank[:],
                lhsT=side_lhsT[:, i, :],
                rhs=side_rows[:, BANK * block : BANK * (block + 1)],
                start=True,
                stop=True,
            )
            side = work.tile([P, BANK], F32, name="side", bufs=SIDE_BUFS)
            nc.scalar.copy(out=side[:], in_=bank[:])
            sides[(i, block)] = side

        side_order = [(i, block) for i in (2, 3, 0, 1, 4, 5) for block in range(BLOCKS)]

        def next_side_terms(count):
            for i, block in side_order[len(sides) : len(sides) + count]:
                side_term(i, block)

        def quantise_group(units, g, codes, scales, copier):
            words = units[:].bitcast(F32)
            turned = psum_aux.tile([P, PACK, P], F32, name="turned", tag="aux")
            for t in range(PACK):
                nc.tensor.transpose(turned[:, t, :], words[:, K_PASS * g + t : K_PASS * (g + 1) : PACK], ident_words[:])
            grouped = work.tile([P, N_VAR, P, PACK], BF16, name="grouped", bufs=2, align_bytes=64)
            halves = turned[:].rearrange("p t b -> p (t b)").bitcast(BF16)
            copier(out=grouped[:], in_=halves.rearrange("p (t b v) -> p v b t", t=PACK, v=N_VAR))
            nc.vector.quantize_mx(
                out=codes[:, g, :].bitcast(FP8X4),
                scales=scales[:, g, :],
                in_=grouped[:].rearrange("p v b t -> p (v b t)"),
            )

        h_codes = const.tile([P, GROUPS, N_VAR * P], U32, name="h_codes", align_bytes=64)
        h_scales = const.tile([P, GROUPS, N_VAR * P], U8, name="h_scales", align_bytes=64)
        hr = const.tile([P, UNITS], BF16, name="hr")
        hr_codes = const.tile([P, GROUPS, N_VAR * P], U32, name="hr_codes", align_bytes=64)
        hr_scales = const.tile([P, GROUPS, N_VAR * P], U8, name="hr_scales", align_bytes=64)

        def mx_pass(acc, codes, scales, v, g, w_cols, plane_cols):
            nc.tensor.matmul_mx(
                out=acc[:],
                lhsT=codes[:, g, v * P : (v + 1) * P].bitcast(FP8X4),
                lhsT_scale=scales[:, g, v * P : (v + 1) * P],
                rhs=w_cols.bitcast(FP8X4),
                rhs_scale=plane_cols,
                start=(g == 0),
                stop=(g == GROUPS - 1),
            )

        def add_side(acc, side):
            pre = work.tile([P, BANK], F32, name="pre", bufs=BLOCKS + 2)
            nc.vector.tensor_tensor(out=pre[:], in0=acc[:], in1=side[:], op=ALU.add)
            return pre

        def two_side_terms(g):
            next_side_terms(1)

        def gate_range(v, half, after_group=two_side_terms):
            accs = [psum_mx.tile([P, BANK], F32, name="acc") for block in range(BLOCKS)]
            for g in range(GROUPS):
                w = next_weights()
                for block in range(BLOCKS):
                    col = RANGE * half + BANK * block
                    mx_pass(
                        accs[block], h_codes, h_scales, v, g,
                        w[:, BANK * block : BANK * (block + 1)],
                        gate_planes[v][PACK * g : P, col : col + BANK],
                    )
                after_group(g)
            return [add_side(accs[block], sides[(HALVES * v + half, block)]) for block in range(BLOCKS)]

        def activated(pre, func, scale):
            act = work.tile([P, BANK], F32, name="act")
            nc.scalar.activation(out=act[:], in_=pre[:], func=func, scale=scale)
            return act

        def reset_product(half, pres):
            for block in range(BLOCKS):
                reset = activated(pres[block], ACT.Sigmoid, 1.0)
                cols = slice(RANGE * half + BANK * block, RANGE * half + BANK * (block + 1))
                nc.vector.tensor_tensor(out=hr[:, cols], in0=hidden_sb[:, cols], in1=reset[:], op=ALU.mult)

        def quantise_product(pair):
            for g in (2 * pair, 2 * pair + 1):
                quantise_group(hr, g, hr_codes, hr_scales, nc.scalar.copy)

        keep = const.tile([P, UNITS], F32, name="keep")
        fresh = const.tile([P, UNITS], F32, name="fresh")

        def update_gate(half, pres):
            for block in range(BLOCKS):
                cols = slice(RANGE * half + BANK * block, RANGE * half + BANK * (block + 1))
                update = activated(pres[block], ACT.Sigmoid, 1.0)
                nc.vector.tensor_tensor(out=keep[:, cols], in0=update[:], in1=hidden_sb[:, cols], op=ALU.mult)
            for block in range(BLOCKS):
                cols = slice(RANGE * half + BANK * block, RANGE * half + BANK * (block + 1))
                nc.scalar.activation(out=fresh[:, cols], in_=pres[block][:], func=ACT.Sigmoid, scale=-1.0)

        def first_side_terms(g):
            if g == 1:
                turn_inputs()
            if g >= 2:
                next_side_terms(BLOCKS)

        for g in range(GROUPS):
            quantise_group(hidden_sb, g, h_codes, h_scales, nc.scalar.copy if g % 2 == 0 else nc.vector.tensor_copy)
        update_planes = load_planes("update_planes", gate_w_H2H_scales, 0, False)
        gate_planes = [update_planes, reset_planes]
        cand_planes = [load_planes("cand_planes%d" % v, update_w_H2H_scales, v, False) for v in range(N_VAR)]
        place_inputs()
        reset_product(0, gate_range(1, 0, first_side_terms))
        reset_product(1, gate_range(1, 1))
        quantise_product(0)
        update_gate(0, gate_range(0, 0))
        quantise_product(1)
        update_gate(1, gate_range(0, 1))

        def blend(cols, cand):
            mixed = work.tile([P, BANK], F32, name="mixed", bufs=2)
            nc.vector.tensor_tensor(out=mixed[:], in0=cand[:], in1=fresh[:, cols], op=ALU.mult)
            nc.vector.tensor_tensor(out=keep[:, cols], in0=mixed[:], in1=keep[:, cols], op=ALU.add)
            nc.sync.dma_start(out=out[:, cols], in_=keep[:, cols])

        def candidate_quarter(q):
            v = q // 2
            accs = [psum_mx.tile([P, BANK], F32, name="acc") for block in range(2)]
            for s in range(2):
                w = next_weights()
                for g in (2 * s, 2 * s + 1):
                    for block in range(2):
                        first = QUARTER * (g % 2) + BANK * block
                        col = QUARTER * (q % 2) + BANK * block
                        mx_pass(
                            accs[block], hr_codes, hr_scales, v, g,
                            w[:, first : first + BANK],
                            cand_planes[v][PACK * g : P, col : col + BANK],
                        )
                next_side_terms(1)
            pres = [add_side(accs[block], sides[(gate_ranges + v, 2 * (q % 2) + block)]) for block in range(2)]
            cands = [activated(pres[block], ACT.Tanh, 1.0) for block in range(2)]
            mixeds = []
            for block in range(2):
                cols = slice(QUARTER * q + BANK * block, QUARTER * q + BANK * (block + 1))
                mixed = work.tile([P, BANK], F32, name="mixed", bufs=2)
                nc.vector.tensor_tensor(out=mixed[:], in0=cands[block][:], in1=fresh[:, cols], op=ALU.mult)
                mixeds.append(mixed)
            for block in range(2):
                cols = slice(QUARTER * q + BANK * block, QUARTER * q + BANK * (block + 1))
                nc.vector.tensor_tensor(out=keep[:, cols], in0=mixeds[block][:], in1=keep[:, cols], op=ALU.add)
            nc.sync.dma_start(out=out[:, QUARTER * q : QUARTER * (q + 1)], in_=keep[:, QUARTER * q : QUARTER * (q + 1)])

        for q in range(QUARTERS - 1):
            candidate_quarter(q)

        waiting = []
        for v in (1,):
            for block in (2, 3):
                w = next_weights()
                acc = psum_mx.tile([P, BANK], F32, name="acc")
                for g in range(GROUPS):
                    mx_pass(
                        acc, hr_codes, hr_scales, v, g,
                        w[:, BANK * g : BANK * (g + 1)],
                        cand_planes[v][PACK * g : P, BANK * block : BANK * (block + 1)],
                    )
                cand = activated(add_side(acc, sides[(gate_ranges + v, block)]), ACT.Tanh, 1.0)
                for cols, earlier in waiting:
                    blend(cols, earlier)
                waiting = [(slice(D * v + BANK * block, D * v + BANK * (block + 1)), cand)]
        for cols, earlier in waiting:
            blend(cols, earlier)
